import numpy as np
import ml_dtypes


def mxq(x, axis, fmt="e4m3"):
    dtype, down = {"e4m3": (ml_dtypes.float8_e4m3fn, 7), "e5m2": (ml_dtypes.float8_e5m2, 14)}[fmt]
    v = np.moveaxis(np.asarray(x, np.float32).astype(ml_dtypes.bfloat16).astype(np.float64), axis, -1)
    blocks = v.reshape(v.shape[:-1] + (-1, 32))
    amax = np.abs(blocks).max(-1, keepdims=True)
    byte = np.maximum(np.where(amax > 0, np.frexp(amax)[1] - 1 + 127, 0) - down, 1)
    scale = np.exp2(byte - 127.0)
    codes = (blocks / scale).astype(np.float32).astype(dtype).astype(np.float64)
    return np.moveaxis((codes * scale).reshape(v.shape), -1, axis)


WIDE = False


def mx_kscale(k):
    if not WIDE:
        return np.ones(k)
    levels = np.array([18, -18])
    if k % 512:
        return np.exp2(np.random.permutation(np.resize(levels, k // 32))).repeat(32)
    a = np.empty((k // 512, 16))
    for p in range(k // 512):
        a[p, :8] = np.random.permutation(np.resize(levels, 8))
        for g in range(8):
            far = levels[np.abs(levels - a[p, g]) >= 10]
            a[p, g + 8] = far[np.random.randint(len(far))]
    return np.exp2(a.ravel()).repeat(32)


BF16 = ml_dtypes.bfloat16


def bf(x):
    return np.asarray(x, np.float32).astype(BF16)


def f64(x):
    return np.asarray(x).astype(np.float64)


B, S, E, H, DK = 2, 512, 1024, 8, 128
HD = H * DK
T = B * S


def rotate_half(u):
    shp = u.shape
    u = u.reshape(shp[:-1] + (shp[-1] // 2, 2))
    u1, u2 = u[..., 0], u[..., 1]
    return np.stack((-u2, u1), axis=-1).reshape(shp)


def setup_inputs():
    s = mx_kscale(T)
    uq = mx_kscale(HD)
    uk = mx_kscale(HD)
    theta = np.repeat(np.random.uniform(-np.pi, np.pi, (S, DK // 2)), 2, axis=-1)
    st = s.reshape(B, 1, S, 1)
    x = bf(np.random.standard_normal((B, S, E)) * s.reshape(B, S, 1))
    wq = bf(np.random.standard_normal((HD, E)) / np.sqrt(E) / uq[:, None])
    wk = bf(np.random.standard_normal((HD, E)) / np.sqrt(E) / uk[:, None])
    g0 = bf(np.random.standard_normal((B, H, S, DK)) * np.exp2(np.random.randint(-6, 1, (B, 1, S, 1))) / st * uq.reshape(1, H, 1, DK))
    g1 = bf(np.random.standard_normal((B, H, S, DK)) * np.exp2(np.random.randint(-6, 1, (B, 1, S, 1))) / st * uk.reshape(1, H, 1, DK))
    return {"x": x, "wq": wq, "wk": wk,
            "cos_tab": bf(np.cos(theta)),
            "sin_tab": bf(np.sin(theta)),
            "grad_0": g0, "grad_1": g1}


def reference(x, wq, wk, cos_tab, sin_tab, grad_0, grad_1):
    c, sn = f64(cos_tab), f64(sin_tab)

    def unrot(g):
        d = g * c - rotate_half(g * sn)
        return d.transpose(0, 2, 1, 3).reshape(T, HD)

    dz = np.concatenate([unrot(f64(grad_0)), unrot(f64(grad_1))], axis=1)
    w = np.concatenate([f64(wq), f64(wk)], axis=0)
    dx = mxq(dz, 1, "e5m2") @ mxq(w, 0, "e4m3")
    xq = mxq(f64(x).reshape(T, E), 0, "e4m3")
    dw = mxq(dz, 0, "e5m2").T @ xq
    return dx.reshape(B, S, E), dw[:HD], dw[HD:]

@@ -1,0 +1,318 @@
+from contextlib import ExitStack
+
+import concourse.mybir as mybir
+from concourse.masks import make_identity
+
+B, S, E, H, DK = 2, 512, 1024, 8, 128
+HD = H * DK
+FLOPS = 2 * (B * S) * (2 * HD) * E * 2
+
+F32 = mybir.dt.float32
+BF16 = mybir.dt.bfloat16
+U32 = mybir.dt.uint32
+U8 = mybir.dt.uint8
+E4M3 = mybir.dt.float8_e4m3fn_x4
+E5M2 = mybir.dt.float8_e5m2_x4
+MULT = mybir.AluOpType.mult
+ADD = mybir.AluOpType.add
+
+P = 128
+UNITS = [(0, 0, 0), (0, 1, 0), (1, 0, 0), (1, 1, 0), (0, 0, 1), (1, 0, 1), (0, 1, 1), (1, 1, 1)]
+V_PIECES = {4: 2, 5: 6}
+
+
+def tile_multiheadattention_pa_v_kernel(tc, x, wq, wk, cos_tab, sin_tab, grad_0, grad_1, out_0, out_1, out_2):
+    nc = tc.nc
+    grads = [grad_0, grad_1]
+    weights = [wq, wk]
+    w_outs = [out_1, out_2]
+    with ExitStack() as ctx:
+        const = ctx.enter_context(tc.tile_pool(name="const", bufs=1))
+        gpool = ctx.enter_context(tc.tile_pool(name="gpool", bufs=7))
+        keep = ctx.enter_context(tc.tile_pool(name="keep", bufs=1))
+        grp_pool = ctx.enter_context(tc.tile_pool(name="grp_pool", bufs=3))
+        t_pool = ctx.enter_context(tc.tile_pool(name="t_pool", bufs=3))
+        d_pool = ctx.enter_context(tc.tile_pool(name="d_pool", bufs=3))
+        dt_pool = ctx.enter_context(tc.tile_pool(name="dt_pool", bufs=2))
+        o_pool = ctx.enter_context(tc.tile_pool(name="o_pool", bufs=4))
+        tab_psum = ctx.enter_context(tc.psum_pool(name="tab_psum", bufs=1))
+        tr_psum = ctx.enter_context(tc.psum_pool(name="tr_psum", bufs=2))
+        acc_psum = ctx.enter_context(tc.psum_pool(name="acc_psum", bufs=5))
+        ctx.enter_context(tc.manual_schedule())
+
+        ident = const.tile([P, P], F32, name="ident")
+        ident_bf = const.tile([P, P], BF16, name="ident_bf")
+        make_identity(nc, ident_bf[:])
+        make_identity(nc, ident[:])
+
+        tabs = const.tile([P, 2, 512], BF16, name="tabs")
+        sin_raw = const.tile([P, 512], BF16, name="sin_raw")
+        nc.sync.dma_start(out=tabs[:, 0, :].rearrange("p (j f) -> p j f", j=4), in_=cos_tab.rearrange("(p j) f -> p j f", j=4))
+        nc.sync.dma_start(out=sin_raw[:].rearrange("p (j f) -> p j f", j=4), in_=sin_tab.rearrange("(p j) f -> p j f", j=4))
+        g_raw = {}
+        x_raw = {}
+        w_raw = {}
+
+        def load_g(u):
+            tau, b, g = UNITS[u]
+            t = gpool.tile([P, 4, 512], BF16, name="g_raw")
+            g_raw[u] = t
+            nc.sync.dma_start(
+                out=t[:].rearrange("p h (j f) -> p h j f", j=4),
+                in_=grads[tau][b, 4 * g : 4 * g + 4].rearrange("h (p j) f -> p h j f", j=4),
+            )
+
+        def load_x(b):
+            t = keep.tile([P, 4, E], BF16, name="x_raw%d" % b)
+            x_raw[b] = t
+            for n in range(2):
+                nc.sync.dma_start(
+                    out=t[:, :, 512 * n : 512 * n + 512],
+                    in_=x[b].rearrange("(p j) e -> p j e", j=4)[:, :, 512 * n : 512 * n + 512],
+                )
+
+        def load_w(k):
+            tau, g = k % 2, k // 2
+            t = keep.tile([P, 4, E], BF16, name="w_raw%d" % k)
+            w_raw[k] = t
+            nc.sync.dma_start(out=t[:], in_=weights[tau][512 * g : 512 * g + 512, :].rearrange("(p j) e -> p j e", j=4))
+
+        load_g(0)
+        load_x(0)
+        load_g(1)
+        load_x(1)
+        load_w(0)
+        load_g(2)
+        load_g(3)
+        load_w(1)
+        load_g(4)
+        load_w(2)
+        load_g(5)
+        load_g(6)
+        load_w(3)
+        load_g(7)
+
+        sv = sin_raw[:].rearrange("p (n e) -> p n e", e=2)
+        s2 = tabs[:, 1, :].rearrange("p (n e) -> p n e", e=2)
+        nc.vector.tensor_copy(out=s2[:, :, 0], in_=sv[:, :, 1])
+        nc.vector.tensor_scalar(out=s2[:, :, 1], in0=sv[:, :, 0], scalar1=-1.0, scalar2=None, op0=MULT)
+        tab_t = const.tile([P, 8, P], BF16, name="tab_t")
+        first = tr_psum.tile([P, 8, P], BF16, name="tr")
+        tab_ps = tab_psum.tile([P, 2, 512], BF16, name="tab_ps")
+        tabs_flat = tabs[:].rearrange("p a n -> p (a n)")
+        for k in range(8):
+            nc.tensor.transpose(first[:, k, :], tabs_flat[:, P * k : P * k + P], ident_bf[:])
+        nc.scalar.copy(out=tab_t[:].rearrange("p k n -> p (k n)"), in_=first[:].rearrange("p k n -> p (k n)"))
+        ps_flat = tab_ps[:].rearrange("p a n -> p (a n)")
+        for k in range(8):
+            nc.tensor.transpose(ps_flat[:, P * k : P * k + P], tab_t[:, k, :], ident_bf[:])
+
+        t_tiles = {}
+        d_tiles = {}
+        dq = {}
+        dqs = {}
+        dt_tiles = {}
+        dtq = {}
+        dtqs = {}
+        tr_tiles = {}
+        grp = {}
+        mq = {}
+        mqs = {}
+
+        def mul(c):
+            src = tabs if c == 0 else tab_ps
+            graw = g_raw[c // 2][:, 2 * (c % 2) : 2 * (c % 2) + 2, :]
+            t1 = t_pool.tile([P, 2, 512], F32, name="t1")
+            t2 = t_pool.tile([P, 2, 512], F32, name="t2")
+            t_tiles[c] = (t1, t2)
+            nc.vector.tensor_tensor(out=t1[:], in0=graw, in1=src[:, 0, :].unsqueeze(1).to_broadcast([P, 2, 512]), op=MULT)
+            nc.vector.tensor_tensor(
+                out=t2[:].rearrange("p h (n e) -> p h n e", e=2),
+                in0=graw.rearrange("p h (n e) -> p h n e", e=2)[:, :, :, ::-1],
+                in1=src[:, 1, :].rearrange("p (n e) -> p n e", e=2).unsqueeze(1).to_broadcast([P, 2, 256, 2]),
+                op=MULT,
+            )
+
+        def add(c, h, eng):
+            u = c // 2
+            if c % 2 == 0 and h == 0:
+                d_tiles[u] = d_pool.tile([P, 2048], BF16, name="d_grp", align_bytes=64)
+                dq[u] = keep.tile([P, 512], U32, name="dq%d" % u, align_bytes=64)
+                dqs[u] = keep.tile([P, 512], U8, name="dqs%d" % u, align_bytes=64)
+            t1, t2 = t_tiles[c]
+            o = 1024 * (c % 2) + 512 * h
+            eng.tensor_tensor(
+                out=d_tiles[u][:, o : o + 512].rearrange("p (f j) -> p f j", j=4),
+                in0=t1[:, h, :].rearrange("p (j f) -> p f j", j=4),
+                in1=t2[:, h, :].rearrange("p (j f) -> p f j", j=4),
+                op=ADD,
+            )
+
+        def quant_d(c):
+            u, hf = c // 2, c % 2
+            nc.vector.quantize_mx(
+                out=dq[u][:, 256 * hf : 256 * hf + 256].bitcast(E5M2),
+                scales=dqs[u][:, 256 * hf : 256 * hf + 256],
+                in_=d_tiles[u][:, 1024 * hf : 1024 * hf + 1024],
+            )
+
+        def flip(u, jj):
+            words = d_tiles[u][:].bitcast(F32).rearrange("p (q t w) -> p t w q", t=4, w=2)
+            tr = tr_psum.tile([P, 4, P], F32, name="tr")
+            tr_tiles[(u, jj)] = tr
+            for t in range(4):
+                nc.tensor.transpose(tr[:, t, :], words[:, t, jj, :], ident[:])
+
+        def unflip(u, jj, copy):
+            if jj == 0:
+                dt_tiles[u] = dt_pool.tile([P, 2048], BF16, name="dt", align_bytes=64)
+                dtq[u] = keep.tile([P, 512], U32, name="dtq%d" % u, align_bytes=64)
+                dtqs[u] = keep.tile([P, 512], U8, name="dtqs%d" % u, align_bytes=64)
+            tr = tr_tiles[(u, jj)]
+            copy(
+                out=dt_tiles[u][:, 1024 * jj : 1024 * jj + 1024].rearrange("q (e p t) -> q e p t", e=2, t=4),
+                in_=tr[:].rearrange("q t p -> q (t p)").bitcast(BF16).rearrange("q (t p e) -> q e p t", t=4, e=2),
+            )
+
+        def quant_dt(u, jj):
+            nc.vector.quantize_mx(
+                out=dtq[u][:, 256 * jj : 256 * jj + 256].bitcast(E5M2),
+                scales=dtqs[u][:, 256 * jj : 256 * jj + 256],
+                in_=dt_tiles[u][:, 1024 * jj : 1024 * jj + 1024],
+            )
+
+        def inter(i, copy, c0=0, c1=512):
+            src = x_raw[i // 2] if i < 4 else w_raw[(i - 4) // 2]
+            if c0 == 0:
+                grp[i] = grp_pool.tile([P, 2048], BF16, name="grp", align_bytes=64)
+            n0 = 512 * (i % 2)
+            copy(
+                out=grp[i][:, 4 * c0 : 4 * c1].rearrange("p (c i j) -> p c j i", i=4, j=4),
+                in_=src[:, :, n0 + c0 : n0 + c1].rearrange("p j (c i) -> p c j i", i=4),
+            )
+
+        def quant_m(i):
+            mq[i] = keep.tile([P, 512], U32, name="mq%d" % i, align_bytes=64)
+            mqs[i] = keep.tile([P, 512], U8, name="mqs%d" % i, align_bytes=64)
+            nc.vector.quantize_mx(out=mq[i][:].bitcast(E4M3), scales=mqs[i][:], in_=grp[i][:])
+
+        acc = {}
+        o_tiles = {}
+
+        def mm(job, p0, p1):
+            ps = passes_of(job)
+            if p0 == 0:
+                acc[job] = acc_psum.tile([P, 512], F32, name="acc")
+            for i in range(p0, p1):
+                q, qs, m, rhs = one_pass(job, i)
+                nc.tensor.matmul_mx(
+                    out=acc[job][:],
+                    lhsT=q[:, P * m : P * m + P].bitcast(E5M2),
+                    lhsT_scale=qs[:, P * m : P * m + P],
+                    rhs=mq[rhs][:].bitcast(E4M3),
+                    rhs_scale=mqs[rhs][:],
+                    start=(i == 0),
+                    stop=(i == ps - 1),
+                )
+
+        def passes_of(job):
+            return 2 if job[0] == "W" else 4
+
+        def one_pass(job, i):
+            kind, a, m, n = job
+            if kind == "W":
+                u = [u for u in range(8) if UNITS[u][0] == a % 2 and UNITS[u][2] == a // 2][i]
+                return dq[u], dqs[u], m, 2 * UNITS[u][1] + n
+            u = [u for u in range(8) if UNITS[u][1] == a][i]
+            return dtq[u], dtqs[u], m, 4 + 2 * (UNITS[u][0] + 2 * UNITS[u][2]) + n
+
+        def dst(job):
+            kind, a, m, n = job
+            if kind == "W":
+                r = 512 * (a // 2) + P * m
+                return w_outs[a % 2][r : r + P, :]
+            return out_0[a].rearrange("(p j) e -> j p e", j=4)[m]
+
+        def drain(job, copy, alone):
+            key = job[:3]
+            n = job[3]
+            if job[0] == "X":
+                o = o_pool.tile([P, 512], F32, name="ox")
+                copy(out=o[:], in_=acc[job][:])
+                nc.sync.dma_start(out=dst(job)[:, 512 * n : 512 * n + 512], in_=o[:])
+                return
+            if key not in o_tiles:
+                o_tiles[key] = [o_pool.tile([P, E], F32, name="o"), 0]
+            o = o_tiles[key][0]
+            cols = slice(512 * n, 512 * n + 512)
+            copy(out=o[:, cols], in_=acc[job][:])
+            o_tiles[key][1] += 1
+            if alone:
+                nc.sync.dma_start(out=dst(job)[:, cols], in_=o[:, cols])
+            elif o_tiles[key][1] == 2:
+                nc.sync.dma_start(out=dst(job), in_=o[:])
+
+        def w_jobs(a, hf):
+            return [("W", a, 2 * hf + i, n) for i in range(2) for n in range(2)]
+
+        def x_jobs(b, n, js=range(4)):
+            return [("X", b, j, n) for j in js]
+
+        pe = {s: [] for s in range(20)}
+        pe[4] = [(j, 0, 2) for j in w_jobs(0, 0)]
+        pe[5] = [(j, 0, 2) for j in w_jobs(0, 1)]
+        pe[8] = [(j, 0, 2) for j in w_jobs(1, 0)]
+        pe[9] = [(j, 0, 2) for j in w_jobs(1, 1)]
+        pe[11] = [(j, 0, 2) for j in x_jobs(0, 0)]
+        pe[12] = [(j, 2, 3) for j in x_jobs(0, 0)]
+        pe[14] = [(j, 3, 4) for j in x_jobs(0, 0)] + [(j, 0, 2) for j in w_jobs(2, 0)] + [(j, 0, 4) for j in x_jobs(0, 1, range(2))]
+        pe[15] = [(j, 0, 2) for j in w_jobs(2, 1)] + [(j, 0, 4) for j in x_jobs(0, 1, range(2, 4))] + [(j, 0, 2) for j in w_jobs(3, 0)]
+        pe[16] = [(j, 0, 3) for j in x_jobs(1, 0)]
+        pe[17] = [(j, 0, 2) for j in w_jobs(3, 1)] + [(j, 3, 4) for j in x_jobs(1, 0)] + [(j, 0, 4) for j in x_jobs(1, 1)]
+
+        s_pieces = {-1: [0], 0: [1], 1: [2], 2: [3], 3: [6], 4: [7], 5: [], 6: [8], 7: [9], 9: [10], 10: [11]}
+        q_pieces = {1: [0, 1], 2: [2], 3: [3], 4: [4, 6], 5: [7], 8: [5, 8], 9: [9], 11: [10], 12: [11]}
+        v_half = {}
+        for i, s in V_PIECES.items():
+            v_half[s] = (i, 0)
+            v_half[s + 1] = (i, 256)
+
+        for i in s_pieces[-1]:
+            inter(i, nc.scalar.copy)
+        turn = 0
+        for c in range(18):
+            if c < 16:
+                mul(c)
+                for h in range(2):
+                    add(c, h, nc.vector if (c == 15 and h == 1) else nc.gpsimd)
+            if 1 <= c <= 16:
+                quant_d(c - 1)
+            if c in v_half:
+                i, c0 = v_half[c]
+                inter(i, nc.vector.tensor_copy, c0, c0 + 256)
+            for i in q_pieces.get(c, []):
+                quant_m(i)
+            for i in s_pieces.get(c, []):
+                inter(i, nc.scalar.copy)
+            if c == 16:
+                flip(7, 0)
+                flip(7, 1)
+                unflip(7, 0, nc.scalar.copy)
+                unflip(7, 1, nc.vector.tensor_copy)
+                quant_dt(7, 0)
+                quant_dt(7, 1)
+            for job, p0, p1 in pe[c]:
+                mm(job, p0, p1)
+                if p1 == passes_of(job):
+                    on_v = c >= 16 and turn % 2 == 1
+                    turn += 1
+                    drain(job, nc.vector.tensor_copy if on_v else nc.scalar.copy, c >= 17)
+            if c % 2 == 0 and 2 <= c < 16:
+                u = c // 2 - 1
+                for jj in range(2):
+                    flip(u, jj)
+                for jj in range(2):
+                    unflip(u, jj, nc.scalar.copy)
+            if c % 2 == 1 and 3 <= c < 16:
+                for jj in range(2):
+                    quant_dt((c - 3) // 2, jj)

@@ -18,7 +18,21 @@ ADD = mybir.AluOpType.add
 
 P = 128
 UNITS = [(0, 0, 0), (0, 1, 0), (1, 0, 0), (1, 1, 0), (0, 0, 1), (1, 0, 1), (0, 1, 1), (1, 1, 1)]
-V_PIECES = {4: 2, 5: 6}
+LOADS = ["g0", "x0", "g1", "x1", "w0", "g2", "g3", "w1", "g4", "w2", "g5", "g6", "w3", "g7"]
+S_INT = {-1: [0], 0: [2], 1: [3], 3: [4], 4: [5], 5: [6], 6: [7], 7: [8], 8: [9], 9: [10], 11: [11]}
+V_INT = {1: [1]}
+Q_INT = {1: [0], 2: [1, 2], 3: [3], 5: [4], 6: [5], 7: [6], 8: [7], 9: [8], 10: [9], 11: [10], 13: [11]}
+PE = {
+    5: [("W", 0, 0, 0, 2)],
+    6: [("W", 0, 1, 0, 2)],
+    9: [("W", 1, 0, 0, 2)],
+    10: [("W", 1, 1, 0, 2)],
+    12: [("X", 0, 0, 0, 2)],
+    13: [("X", 0, 0, 2, 3)],
+    14: [("W", 2, 0, 0, 2)],
+    15: [("X", 0, 0, 3, 4), ("W", 2, 1, 0, 2), ("X", 0, 1, 0, 4)],
+}
+V_OUT_FROM = 12
 
 
 def tile_multiheadattention_pa_v_kernel(tc, x, wq, wk, cos_tab, sin_tab, grad_0, grad_1, out_0, out_1, out_2):
@@ -28,13 +42,14 @@ def tile_multiheadattention_pa_v_kernel(tc, x, wq, wk, cos_tab, sin_tab, grad_0,
     w_outs = [out_1, out_2]
     with ExitStack() as ctx:
         const = ctx.enter_context(tc.tile_pool(name="const", bufs=1))
-        gpool = ctx.enter_context(tc.tile_pool(name="gpool", bufs=7))
+        gpool = ctx.enter_context(tc.tile_pool(name="gpool", bufs=6))
         keep = ctx.enter_context(tc.tile_pool(name="keep", bufs=1))
         grp_pool = ctx.enter_context(tc.tile_pool(name="grp_pool", bufs=3))
-        t_pool = ctx.enter_context(tc.tile_pool(name="t_pool", bufs=3))
+        t_pool = ctx.enter_context(tc.tile_pool(name="t_pool", bufs=2))
         d_pool = ctx.enter_context(tc.tile_pool(name="d_pool", bufs=3))
         dt_pool = ctx.enter_context(tc.tile_pool(name="dt_pool", bufs=2))
         o_pool = ctx.enter_context(tc.tile_pool(name="o_pool", bufs=4))
+        ox_pool = ctx.enter_context(tc.tile_pool(name="ox_pool", bufs=8))
         tab_psum = ctx.enter_context(tc.psum_pool(name="tab_psum", bufs=1))
         tr_psum = ctx.enter_context(tc.psum_pool(name="tr_psum", bufs=2))
         acc_psum = ctx.enter_context(tc.psum_pool(name="acc_psum", bufs=5))
@@ -50,47 +65,32 @@ def tile_multiheadattention_pa_v_kernel(tc, x, wq, wk, cos_tab, sin_tab, grad_0,
         nc.sync.dma_start(out=tabs[:, 0, :].rearrange("p (j f) -> p j f", j=4), in_=cos_tab.rearrange("(p j) f -> p j f", j=4))
         nc.sync.dma_start(out=sin_raw[:].rearrange("p (j f) -> p j f", j=4), in_=sin_tab.rearrange("(p j) f -> p j f", j=4))
         g_raw = {}
-        x_raw = {}
-        w_raw = {}
+        raw = {}
 
         def load_g(u):
             tau, b, g = UNITS[u]
-            t = gpool.tile([P, 4, 512], BF16, name="g_raw")
-            g_raw[u] = t
+            g_raw[u] = gpool.tile([P, 4, 512], BF16, name="g_raw")
             nc.sync.dma_start(
-                out=t[:].rearrange("p h (j f) -> p h j f", j=4),
+                out=g_raw[u][:].rearrange("p h (j f) -> p h j f", j=4),
                 in_=grads[tau][b, 4 * g : 4 * g + 4].rearrange("h (p j) f -> p h j f", j=4),
             )
 
         def load_x(b):
-            t = keep.tile([P, 4, E], BF16, name="x_raw%d" % b)
-            x_raw[b] = t
+            raw[b] = keep.tile([P, 4, E], BF16, name="raw%d" % b)
             for n in range(2):
                 nc.sync.dma_start(
-                    out=t[:, :, 512 * n : 512 * n + 512],
+                    out=raw[b][:, :, 512 * n : 512 * n + 512],
                     in_=x[b].rearrange("(p j) e -> p j e", j=4)[:, :, 512 * n : 512 * n + 512],
                 )
 
         def load_w(k):
-            tau, g = k % 2, k // 2
-            t = keep.tile([P, 4, E], BF16, name="w_raw%d" % k)
-            w_raw[k] = t
-            nc.sync.dma_start(out=t[:], in_=weights[tau][512 * g : 512 * g + 512, :].rearrange("(p j) e -> p j e", j=4))
+            raw[2 + k] = keep.tile([P, 4, E], BF16, name="raw%d" % (2 + k))
+            w = weights[k % 2]
+            g = k // 2
+            nc.sync.dma_start(out=raw[2 + k][:], in_=w[512 * g : 512 * g + 512, :].rearrange("(p j) e -> p j e", j=4))
 
-        load_g(0)
-        load_x(0)
-        load_g(1)
-        load_x(1)
-        load_w(0)
-        load_g(2)
-        load_g(3)
-        load_w(1)
-        load_g(4)
-        load_w(2)
-        load_g(5)
-        load_g(6)
-        load_w(3)
-        load_g(7)
+        for item in LOADS:
+            {"g": load_g, "x": load_x, "w": load_w}[item[0]](int(item[1]))
 
         sv = sin_raw[:].rearrange("p (n e) -> p n e", e=2)
         s2 = tabs[:, 1, :].rearrange("p (n e) -> p n e", e=2)
@@ -119,45 +119,52 @@ def tile_multiheadattention_pa_v_kernel(tc, x, wq, wk, cos_tab, sin_tab, grad_0,
         mq = {}
         mqs = {}
 
-        def mul(c):
+        def heads_of(c):
+            return g_raw[c // 2][:, 2 * (c % 2) : 2 * (c % 2) + 2, :]
+
+        def mul_cos(c):
             src = tabs if c == 0 else tab_ps
-            graw = g_raw[c // 2][:, 2 * (c % 2) : 2 * (c % 2) + 2, :]
             t1 = t_pool.tile([P, 2, 512], F32, name="t1")
             t2 = t_pool.tile([P, 2, 512], F32, name="t2")
             t_tiles[c] = (t1, t2)
-            nc.vector.tensor_tensor(out=t1[:], in0=graw, in1=src[:, 0, :].unsqueeze(1).to_broadcast([P, 2, 512]), op=MULT)
+            nc.vector.tensor_tensor(out=t1[:], in0=heads_of(c), in1=src[:, 0, :].unsqueeze(1).to_broadcast([P, 2, 512]), op=MULT)
+
+        def mul_sin(c, a, b):
+            src = tabs if c == 0 else tab_ps
+            n = (b - a) // 2
             nc.vector.tensor_tensor(
-                out=t2[:].rearrange("p h (n e) -> p h n e", e=2),
-                in0=graw.rearrange("p h (n e) -> p h n e", e=2)[:, :, :, ::-1],
-                in1=src[:, 1, :].rearrange("p (n e) -> p n e", e=2).unsqueeze(1).to_broadcast([P, 2, 256, 2]),
+                out=t_tiles[c][1][:, :, a:b].rearrange("p h (n e) -> p h n e", e=2),
+                in0=heads_of(c)[:, :, a:b].rearrange("p h (n e) -> p h n e", e=2)[:, :, :, ::-1],
+                in1=src[:, 1, a:b].rearrange("p (n e) -> p n e", e=2).unsqueeze(1).to_broadcast([P, 2, n, 2]),
                 op=MULT,
             )
 
-        def add(c, h, eng):
+        def add(c, h0, h1, eng):
             u = c // 2
-            if c % 2 == 0 and h == 0:
-                d_tiles[u] = d_pool.tile([P, 2048], BF16, name="d_grp", align_bytes=64)
+            if u not in d_tiles:
+                d_tiles[u] = d_pool.tile([P, 4, 512], BF16, name="d_grp", align_bytes=64)
                 dq[u] = keep.tile([P, 512], U32, name="dq%d" % u, align_bytes=64)
                 dqs[u] = keep.tile([P, 512], U8, name="dqs%d" % u, align_bytes=64)
             t1, t2 = t_tiles[c]
-            o = 1024 * (c % 2) + 512 * h
-            eng.tensor_tensor(
-                out=d_tiles[u][:, o : o + 512].rearrange("p (f j) -> p f j", j=4),
-                in0=t1[:, h, :].rearrange("p (j f) -> p f j", j=4),
-                in1=t2[:, h, :].rearrange("p (j f) -> p f j", j=4),
-                op=ADD,
-            )
+            o = 2 * (c % 2)
+            for h in range(h0, h1):
+                eng.tensor_tensor(
+                    out=d_tiles[u][:, o + h, :].rearrange("p (c i j) -> p c j i", i=4, j=4),
+                    in0=t1[:, h, :].rearrange("p (j c i) -> p c j i", j=4, i=4),
+                    in1=t2[:, h, :].rearrange("p (j c i) -> p c j i", j=4, i=4),
+                    op=ADD,
+                )
 
         def quant_d(c):
             u, hf = c // 2, c % 2
             nc.vector.quantize_mx(
                 out=dq[u][:, 256 * hf : 256 * hf + 256].bitcast(E5M2),
                 scales=dqs[u][:, 256 * hf : 256 * hf + 256],
-                in_=d_tiles[u][:, 1024 * hf : 1024 * hf + 1024],
+                in_=d_tiles[u][:, 2 * hf : 2 * hf + 2, :].rearrange("p h n -> p (h n)"),
             )
 
         def flip(u, jj):
-            words = d_tiles[u][:].bitcast(F32).rearrange("p (q t w) -> p t w q", t=4, w=2)
+            words = d_tiles[u][:].rearrange("p h n -> p (h n)").bitcast(F32).rearrange("p (q t w) -> p t w q", t=4, w=2)
             tr = tr_psum.tile([P, 4, P], F32, name="tr")
             tr_tiles[(u, jj)] = tr
             for t in range(4):
@@ -174,21 +181,19 @@ def tile_multiheadattention_pa_v_kernel(tc, x, wq, wk, cos_tab, sin_tab, grad_0,
                 in_=tr[:].rearrange("q t p -> q (t p)").bitcast(BF16).rearrange("q (t p e) -> q e p t", t=4, e=2),
             )
 
-        def quant_dt(u, jj):
+        def quant_dt(u, j0, j1):
             nc.vector.quantize_mx(
-                out=dtq[u][:, 256 * jj : 256 * jj + 256].bitcast(E5M2),
-                scales=dtqs[u][:, 256 * jj : 256 * jj + 256],
-                in_=dt_tiles[u][:, 1024 * jj : 1024 * jj + 1024],
+                out=dtq[u][:, 256 * j0 : 256 * j1].bitcast(E5M2),
+                scales=dtqs[u][:, 256 * j0 : 256 * j1],
+                in_=dt_tiles[u][:, 1024 * j0 : 1024 * j1],
             )
 
-        def inter(i, copy, c0=0, c1=512):
-            src = x_raw[i // 2] if i < 4 else w_raw[(i - 4) // 2]
-            if c0 == 0:
-                grp[i] = grp_pool.tile([P, 2048], BF16, name="grp", align_bytes=64)
+        def inter(i, copy):
+            grp[i] = grp_pool.tile([P, 2048], BF16, name="grp", align_bytes=64)
             n0 = 512 * (i % 2)
             copy(
-                out=grp[i][:, 4 * c0 : 4 * c1].rearrange("p (c i j) -> p c j i", i=4, j=4),
-                in_=src[:, :, n0 + c0 : n0 + c1].rearrange("p j (c i) -> p c j i", i=4),
+                out=grp[i][:].rearrange("p (c i j) -> p c j i", i=4, j=4),
+                in_=raw[i // 2][:, :, n0 : n0 + 512].rearrange("p j (c i) -> p c j i", i=4),
             )
 
         def quant_m(i):
@@ -198,22 +203,6 @@ def tile_multiheadattention_pa_v_kernel(tc, x, wq, wk, cos_tab, sin_tab, grad_0,
 
         acc = {}
         o_tiles = {}
-
-        def mm(job, p0, p1):
-            ps = passes_of(job)
-            if p0 == 0:
-                acc[job] = acc_psum.tile([P, 512], F32, name="acc")
-            for i in range(p0, p1):
-                q, qs, m, rhs = one_pass(job, i)
-                nc.tensor.matmul_mx(
-                    out=acc[job][:],
-                    lhsT=q[:, P * m : P * m + P].bitcast(E5M2),
-                    lhsT_scale=qs[:, P * m : P * m + P],
-                    rhs=mq[rhs][:].bitcast(E4M3),
-                    rhs_scale=mqs[rhs][:],
-                    start=(i == 0),
-                    stop=(i == ps - 1),
-                )
 
         def passes_of(job):
             return 2 if job[0] == "W" else 4
@@ -226,6 +215,21 @@ def tile_multiheadattention_pa_v_kernel(tc, x, wq, wk, cos_tab, sin_tab, grad_0,
             u = [u for u in range(8) if UNITS[u][1] == a][i]
             return dtq[u], dtqs[u], m, 4 + 2 * (UNITS[u][0] + 2 * UNITS[u][2]) + n
 
+        def mm(job, p0, p1):
+            if p0 == 0:
+                acc[job] = acc_psum.tile([P, 512], F32, name="acc")
+            for i in range(p0, p1):
+                q, qs, m, rhs = one_pass(job, i)
+                nc.tensor.matmul_mx(
+                    out=acc[job][:],
+                    lhsT=q[:, P * m : P * m + P].bitcast(E5M2),
+                    lhsT_scale=qs[:, P * m : P * m + P],
+                    rhs=mq[rhs][:].bitcast(E4M3),
+                    rhs_scale=mqs[rhs][:],
+                    start=(i == 0),
+                    stop=(i == passes_of(job) - 1),
+                )
+
         def dst(job):
             kind, a, m, n = job
             if kind == "W":
@@ -236,83 +240,72 @@ def tile_multiheadattention_pa_v_kernel(tc, x, wq, wk, cos_tab, sin_tab, grad_0,
         def drain(job, copy, alone):
             key = job[:3]
             n = job[3]
-            if job[0] == "X":
-                o = o_pool.tile([P, 512], F32, name="ox")
+            cols = slice(512 * n, 512 * n + 512)
+            if job[0] == "X" or alone:
+                o = ox_pool.tile([P, 512], F32, name="ox")
                 copy(out=o[:], in_=acc[job][:])
-                nc.sync.dma_start(out=dst(job)[:, 512 * n : 512 * n + 512], in_=o[:])
+                nc.sync.dma_start(out=dst(job)[:, cols], in_=o[:])
                 return
             if key not in o_tiles:
-                o_tiles[key] = [o_pool.tile([P, E], F32, name="o"), 0]
-            o = o_tiles[key][0]
-            cols = slice(512 * n, 512 * n + 512)
-            copy(out=o[:, cols], in_=acc[job][:])
-            o_tiles[key][1] += 1
-            if alone:
-                nc.sync.dma_start(out=dst(job)[:, cols], in_=o[:, cols])
-            elif o_tiles[key][1] == 2:
-                nc.sync.dma_start(out=dst(job), in_=o[:])
+                o_tiles[key] = o_pool.tile([P, E], F32, name="o")
+                copy(out=o_tiles[key][:, cols], in_=acc[job][:])
+            else:
+                copy(out=o_tiles[key][:, cols], in_=acc[job][:])
+                nc.sync.dma_start(out=dst(job), in_=o_tiles[key][:])
 
-        def w_jobs(a, hf):
-            return [("W", a, 2 * hf + i, n) for i in range(2) for n in range(2)]
+        def jobs_of(kind, a, hf):
+            if kind == "W":
+                return [("W", a, 2 * hf + i, n) for i in range(2) for n in range(2)]
+            return [("X", a, j, hf) for j in range(4)]
 
-        def x_jobs(b, n, js=range(4)):
-            return [("X", b, j, n) for j in js]
-
-        pe = {s: [] for s in range(20)}
-        pe[4] = [(j, 0, 2) for j in w_jobs(0, 0)]
-        pe[5] = [(j, 0, 2) for j in w_jobs(0, 1)]
-        pe[8] = [(j, 0, 2) for j in w_jobs(1, 0)]
-        pe[9] = [(j, 0, 2) for j in w_jobs(1, 1)]
-        pe[11] = [(j, 0, 2) for j in x_jobs(0, 0)]
-        pe[12] = [(j, 2, 3) for j in x_jobs(0, 0)]
-        pe[14] = [(j, 3, 4) for j in x_jobs(0, 0)] + [(j, 0, 2) for j in w_jobs(2, 0)] + [(j, 0, 4) for j in x_jobs(0, 1, range(2))]
-        pe[15] = [(j, 0, 2) for j in w_jobs(2, 1)] + [(j, 0, 4) for j in x_jobs(0, 1, range(2, 4))] + [(j, 0, 2) for j in w_jobs(3, 0)]
-        pe[16] = [(j, 0, 3) for j in x_jobs(1, 0)]
-        pe[17] = [(j, 0, 2) for j in w_jobs(3, 1)] + [(j, 3, 4) for j in x_jobs(1, 0)] + [(j, 0, 4) for j in x_jobs(1, 1)]
-
-        s_pieces = {-1: [0], 0: [1], 1: [2], 2: [3], 3: [6], 4: [7], 5: [], 6: [8], 7: [9], 9: [10], 10: [11]}
-        q_pieces = {1: [0, 1], 2: [2], 3: [3], 4: [4, 6], 5: [7], 8: [5, 8], 9: [9], 11: [10], 12: [11]}
-        v_half = {}
-        for i, s in V_PIECES.items():
-            v_half[s] = (i, 0)
-            v_half[s + 1] = (i, 256)
-
-        for i in s_pieces[-1]:
-            inter(i, nc.scalar.copy)
-        turn = 0
-        for c in range(18):
-            if c < 16:
-                mul(c)
-                for h in range(2):
-                    add(c, h, nc.vector if (c == 15 and h == 1) else nc.gpsimd)
-            if 1 <= c <= 16:
-                quant_d(c - 1)
-            if c in v_half:
-                i, c0 = v_half[c]
-                inter(i, nc.vector.tensor_copy, c0, c0 + 256)
-            for i in q_pieces.get(c, []):
-                quant_m(i)
-            for i in s_pieces.get(c, []):
-                inter(i, nc.scalar.copy)
-            if c == 16:
-                flip(7, 0)
-                flip(7, 1)
-                unflip(7, 0, nc.scalar.copy)
-                unflip(7, 1, nc.vector.tensor_copy)
-                quant_dt(7, 0)
-                quant_dt(7, 1)
-            for job, p0, p1 in pe[c]:
+        def run_jobs(kind, a, hf, p0, p1, v_share=0, alone=False):
+            turn = 0
+            for job in jobs_of(kind, a, hf):
                 mm(job, p0, p1)
                 if p1 == passes_of(job):
-                    on_v = c >= 16 and turn % 2 == 1
-                    turn += 1
-                    drain(job, nc.vector.tensor_copy if on_v else nc.scalar.copy, c >= 17)
-            if c % 2 == 0 and 2 <= c < 16:
-                u = c // 2 - 1
+                    turn += v_share
+                    on_v = turn >= 2
+                    turn %= 2
+                    drain(job, nc.vector.tensor_copy if on_v else nc.scalar.copy, alone)
+
+        for i in S_INT[-1]:
+            inter(i, nc.scalar.copy)
+        for c in range(16):
+            mul_cos(c)
+            mul_sin(c, 0, 448)
+            if c >= 1:
+                quant_d(c - 1)
+            if c % 2 == 0 and c >= 4:
+                quant_dt((c - 4) // 2, 0, 2)
+            for i in V_INT.get(c, []):
+                inter(i, nc.vector.tensor_copy)
+            for i in Q_INT.get(c, []):
+                quant_m(i)
+            mul_sin(c, 448, 512)
+            if c < 15:
+                add(c, 0, 2, nc.gpsimd)
+            else:
+                add(c, 0, 1, nc.gpsimd)
+                add(c, 1, 2, nc.vector)
+            for i in S_INT.get(c, []):
+                inter(i, nc.scalar.copy)
+            for k, a, hf, p0, p1 in PE.get(c, []):
+                run_jobs(k, a, hf, p0, p1, 1 if c >= V_OUT_FROM else 0)
+            if c % 2 == 0 and c >= 2:
                 for jj in range(2):
-                    flip(u, jj)
+                    flip(c // 2 - 1, jj)
                 for jj in range(2):
-                    unflip(u, jj, nc.scalar.copy)
-            if c % 2 == 1 and 3 <= c < 16:
-                for jj in range(2):
-                    quant_dt((c - 3) // 2, jj)
+                    unflip(c // 2 - 1, jj, nc.scalar.copy)
+        quant_dt(6, 0, 2)
+        quant_d(15)
+        flip(7, 0)
+        flip(7, 1)
+        unflip(7, 0, nc.scalar.copy)
+        unflip(7, 1, nc.vector.tensor_copy)
+        run_jobs("W", 3, 0, 0, 2, 1, True)
+        run_jobs("X", 1, 0, 0, 3)
+        quant_dt(7, 0, 1)
+        quant_dt(7, 1, 2)
+        run_jobs("W", 3, 1, 0, 2, 1, True)
+        run_jobs("X", 1, 0, 3, 4, 1)
+        run_jobs("X", 1, 1, 0, 4, 1)

from contextlib import ExitStack

import concourse.mybir as mybir
from concourse.masks import make_identity

B, S, E, H, DK = 2, 512, 1024, 8, 128
HD = H * DK
FLOPS = 2 * (B * S) * (2 * HD) * E * 2

F32 = mybir.dt.float32
BF16 = mybir.dt.bfloat16
U32 = mybir.dt.uint32
U8 = mybir.dt.uint8
E4M3 = mybir.dt.float8_e4m3fn_x4
E5M2 = mybir.dt.float8_e5m2_x4
MULT = mybir.AluOpType.mult
ADD = mybir.AluOpType.add

P = 128
UNITS = [(0, 0, 0), (0, 1, 0), (1, 0, 0), (1, 1, 0), (0, 0, 1), (1, 0, 1), (0, 1, 1), (1, 1, 1)]
LOADS = ["g0", "x0", "g1", "x1", "w0", "g2", "g3", "w1", "g4", "w2", "g5", "g6", "w3", "g7"]
S_INT = {-1: [0], 0: [2], 1: [3], 3: [4], 4: [5], 5: [6], 6: [7], 7: [8], 8: [9], 9: [10], 11: [11]}
V_INT = {1: [1]}
Q_INT = {1: [0], 2: [1, 2], 3: [3], 5: [4], 6: [5], 7: [6], 8: [7], 9: [8], 10: [9], 11: [10], 13: [11]}
PE = {
    5: [("W", 0, 0, 0, 2)],
    6: [("W", 0, 1, 0, 2)],
    9: [("W", 1, 0, 0, 2)],
    10: [("W", 1, 1, 0, 2)],
    12: [("X", 0, 0, 0, 2)],
    13: [("X", 0, 0, 2, 3)],
    14: [("W", 2, 0, 0, 2)],
    15: [("X", 0, 0, 3, 4), ("W", 2, 1, 0, 2), ("X", 0, 1, 0, 4)],
}
V_OUT_FROM = 12


def tile_multiheadattention_pa_v_kernel(tc, x, wq, wk, cos_tab, sin_tab, grad_0, grad_1, out_0, out_1, out_2):
    nc = tc.nc
    grads = [grad_0, grad_1]
    weights = [wq, wk]
    w_outs = [out_1, out_2]
    with ExitStack() as ctx:
        const = ctx.enter_context(tc.tile_pool(name="const", bufs=1))
        gpool = ctx.enter_context(tc.tile_pool(name="gpool", bufs=6))
        keep = ctx.enter_context(tc.tile_pool(name="keep", bufs=1))
        grp_pool = ctx.enter_context(tc.tile_pool(name="grp_pool", bufs=3))
        t_pool = ctx.enter_context(tc.tile_pool(name="t_pool", bufs=2))
        d_pool = ctx.enter_context(tc.tile_pool(name="d_pool", bufs=3))
        dt_pool = ctx.enter_context(tc.tile_pool(name="dt_pool", bufs=2))
        o_pool = ctx.enter_context(tc.tile_pool(name="o_pool", bufs=4))
        ox_pool = ctx.enter_context(tc.tile_pool(name="ox_pool", bufs=8))
        tab_psum = ctx.enter_context(tc.psum_pool(name="tab_psum", bufs=1))
        tr_psum = ctx.enter_context(tc.psum_pool(name="tr_psum", bufs=2))
        acc_psum = ctx.enter_context(tc.psum_pool(name="acc_psum", bufs=5))
        ctx.enter_context(tc.manual_schedule())

        ident = const.tile([P, P], F32, name="ident")
        ident_bf = const.tile([P, P], BF16, name="ident_bf")
        make_identity(nc, ident_bf[:])
        make_identity(nc, ident[:])

        tabs = const.tile([P, 2, 512], BF16, name="tabs")
        sin_raw = const.tile([P, 512], BF16, name="sin_raw")
        nc.sync.dma_start(out=tabs[:, 0, :].rearrange("p (j f) -> p j f", j=4), in_=cos_tab.rearrange("(p j) f -> p j f", j=4))
        nc.sync.dma_start(out=sin_raw[:].rearrange("p (j f) -> p j f", j=4), in_=sin_tab.rearrange("(p j) f -> p j f", j=4))
        g_raw = {}
        raw = {}

        def load_g(u):
            tau, b, g = UNITS[u]
            g_raw[u] = gpool.tile([P, 4, 512], BF16, name="g_raw")
            nc.sync.dma_start(
                out=g_raw[u][:].rearrange("p h (j f) -> p h j f", j=4),
                in_=grads[tau][b, 4 * g : 4 * g + 4].rearrange("h (p j) f -> p h j f", j=4),
            )

        def load_x(b):
            raw[b] = keep.tile([P, 4, E], BF16, name="raw%d" % b)
            for n in range(2):
                nc.sync.dma_start(
                    out=raw[b][:, :, 512 * n : 512 * n + 512],
                    in_=x[b].rearrange("(p j) e -> p j e", j=4)[:, :, 512 * n : 512 * n + 512],
                )

        def load_w(k):
            raw[2 + k] = keep.tile([P, 4, E], BF16, name="raw%d" % (2 + k))
            w = weights[k % 2]
            g = k // 2
            nc.sync.dma_start(out=raw[2 + k][:], in_=w[512 * g : 512 * g + 512, :].rearrange("(p j) e -> p j e", j=4))

        for item in LOADS:
            {"g": load_g, "x": load_x, "w": load_w}[item[0]](int(item[1]))

        sv = sin_raw[:].rearrange("p (n e) -> p n e", e=2)
        s2 = tabs[:, 1, :].rearrange("p (n e) -> p n e", e=2)
        nc.vector.tensor_copy(out=s2[:, :, 0], in_=sv[:, :, 1])
        nc.vector.tensor_scalar(out=s2[:, :, 1], in0=sv[:, :, 0], scalar1=-1.0, scalar2=None, op0=MULT)
        tab_t = const.tile([P, 8, P], BF16, name="tab_t")
        first = tr_psum.tile([P, 8, P], BF16, name="tr")
        tab_ps = tab_psum.tile([P, 2, 512], BF16, name="tab_ps")
        tabs_flat = tabs[:].rearrange("p a n -> p (a n)")
        for k in range(8):
            nc.tensor.transpose(first[:, k, :], tabs_flat[:, P * k : P * k + P], ident_bf[:])
        nc.scalar.copy(out=tab_t[:].rearrange("p k n -> p (k n)"), in_=first[:].rearrange("p k n -> p (k n)"))
        ps_flat = tab_ps[:].rearrange("p a n -> p (a n)")
        for k in range(8):
            nc.tensor.transpose(ps_flat[:, P * k : P * k + P], tab_t[:, k, :], ident_bf[:])

        t_tiles = {}
        d_tiles = {}
        dq = {}
        dqs = {}
        dt_tiles = {}
        dtq = {}
        dtqs = {}
        tr_tiles = {}
        grp = {}
        mq = {}
        mqs = {}

        def heads_of(c):
            return g_raw[c // 2][:, 2 * (c % 2) : 2 * (c % 2) + 2, :]

        def mul_cos(c):
            src = tabs if c == 0 else tab_ps
            t1 = t_pool.tile([P, 2, 512], F32, name="t1")
            t2 = t_pool.tile([P, 2, 512], F32, name="t2")
            t_tiles[c] = (t1, t2)
            nc.vector.tensor_tensor(out=t1[:], in0=heads_of(c), in1=src[:, 0, :].unsqueeze(1).to_broadcast([P, 2, 512]), op=MULT)

        def mul_sin(c, a, b):
            src = tabs if c == 0 else tab_ps
            n = (b - a) // 2
            nc.vector.tensor_tensor(
                out=t_tiles[c][1][:, :, a:b].rearrange("p h (n e) -> p h n e", e=2),
                in0=heads_of(c)[:, :, a:b].rearrange("p h (n e) -> p h n e", e=2)[:, :, :, ::-1],
                in1=src[:, 1, a:b].rearrange("p (n e) -> p n e", e=2).unsqueeze(1).to_broadcast([P, 2, n, 2]),
                op=MULT,
            )

        def add(c, h0, h1, eng):
            u = c // 2
            if u not in d_tiles:
                d_tiles[u] = d_pool.tile([P, 4, 512], BF16, name="d_grp", align_bytes=64)
                dq[u] = keep.tile([P, 512], U32, name="dq%d" % u, align_bytes=64)
                dqs[u] = keep.tile([P, 512], U8, name="dqs%d" % u, align_bytes=64)
            t1, t2 = t_tiles[c]
            o = 2 * (c % 2)
            for h in range(h0, h1):
                eng.tensor_tensor(
                    out=d_tiles[u][:, o + h, :].rearrange("p (c i j) -> p c j i", i=4, j=4),
                    in0=t1[:, h, :].rearrange("p (j c i) -> p c j i", j=4, i=4),
                    in1=t2[:, h, :].rearrange("p (j c i) -> p c j i", j=4, i=4),
                    op=ADD,
                )

        def quant_d(c):
            u, hf = c // 2, c % 2
            nc.vector.quantize_mx(
                out=dq[u][:, 256 * hf : 256 * hf + 256].bitcast(E5M2),
                scales=dqs[u][:, 256 * hf : 256 * hf + 256],
                in_=d_tiles[u][:, 2 * hf : 2 * hf + 2, :].rearrange("p h n -> p (h n)"),
            )

        def flip(u, jj):
            words = d_tiles[u][:].rearrange("p h n -> p (h n)").bitcast(F32).rearrange("p (q t w) -> p t w q", t=4, w=2)
            tr = tr_psum.tile([P, 4, P], F32, name="tr")
            tr_tiles[(u, jj)] = tr
            for t in range(4):
                nc.tensor.transpose(tr[:, t, :], words[:, t, jj, :], ident[:])

        def unflip(u, jj, copy):
            if jj == 0:
                dt_tiles[u] = dt_pool.tile([P, 2048], BF16, name="dt", align_bytes=64)
                dtq[u] = keep.tile([P, 512], U32, name="dtq%d" % u, align_bytes=64)
                dtqs[u] = keep.tile([P, 512], U8, name="dtqs%d" % u, align_bytes=64)
            tr = tr_tiles[(u, jj)]
            copy(
                out=dt_tiles[u][:, 1024 * jj : 1024 * jj + 1024].rearrange("q (e p t) -> q e p t", e=2, t=4),
                in_=tr[:].rearrange("q t p -> q (t p)").bitcast(BF16).rearrange("q (t p e) -> q e p t", t=4, e=2),
            )

        def quant_dt(u, j0, j1):
            nc.vector.quantize_mx(
                out=dtq[u][:, 256 * j0 : 256 * j1].bitcast(E5M2),
                scales=dtqs[u][:, 256 * j0 : 256 * j1],
                in_=dt_tiles[u][:, 1024 * j0 : 1024 * j1],
            )

        def inter(i, copy):
            grp[i] = grp_pool.tile([P, 2048], BF16, name="grp", align_bytes=64)
            n0 = 512 * (i % 2)
            copy(
                out=grp[i][:].rearrange("p (c i j) -> p c j i", i=4, j=4),
                in_=raw[i // 2][:, :, n0 : n0 + 512].rearrange("p j (c i) -> p c j i", i=4),
            )

        def quant_m(i):
            mq[i] = keep.tile([P, 512], U32, name="mq%d" % i, align_bytes=64)
            mqs[i] = keep.tile([P, 512], U8, name="mqs%d" % i, align_bytes=64)
            nc.vector.quantize_mx(out=mq[i][:].bitcast(E4M3), scales=mqs[i][:], in_=grp[i][:])

        acc = {}
        o_tiles = {}

        def passes_of(job):
            return 2 if job[0] == "W" else 4

        def one_pass(job, i):
            kind, a, m, n = job
            if kind == "W":
                u = [u for u in range(8) if UNITS[u][0] == a % 2 and UNITS[u][2] == a // 2][i]
                return dq[u], dqs[u], m, 2 * UNITS[u][1] + n
            u = [u for u in range(8) if UNITS[u][1] == a][i]
            return dtq[u], dtqs[u], m, 4 + 2 * (UNITS[u][0] + 2 * UNITS[u][2]) + n

        def mm(job, p0, p1):
            if p0 == 0:
                acc[job] = acc_psum.tile([P, 512], F32, name="acc")
            for i in range(p0, p1):
                q, qs, m, rhs = one_pass(job, i)
                nc.tensor.matmul_mx(
                    out=acc[job][:],
                    lhsT=q[:, P * m : P * m + P].bitcast(E5M2),
                    lhsT_scale=qs[:, P * m : P * m + P],
                    rhs=mq[rhs][:].bitcast(E4M3),
                    rhs_scale=mqs[rhs][:],
                    start=(i == 0),
                    stop=(i == passes_of(job) - 1),
                )

        def dst(job):
            kind, a, m, n = job
            if kind == "W":
                r = 512 * (a // 2) + P * m
                return w_outs[a % 2][r : r + P, :]
            return out_0[a].rearrange("(p j) e -> j p e", j=4)[m]

        def drain(job, copy, alone):
            key = job[:3]
            n = job[3]
            cols = slice(512 * n, 512 * n + 512)
            if job[0] == "X" or alone:
                o = ox_pool.tile([P, 512], F32, name="ox")
                copy(out=o[:], in_=acc[job][:])
                nc.sync.dma_start(out=dst(job)[:, cols], in_=o[:])
                return
            if key not in o_tiles:
                o_tiles[key] = o_pool.tile([P, E], F32, name="o")
                copy(out=o_tiles[key][:, cols], in_=acc[job][:])
            else:
                copy(out=o_tiles[key][:, cols], in_=acc[job][:])
                nc.sync.dma_start(out=dst(job), in_=o_tiles[key][:])

        def jobs_of(kind, a, hf):
            if kind == "W":
                return [("W", a, 2 * hf + i, n) for i in range(2) for n in range(2)]
            return [("X", a, j, hf) for j in range(4)]

        def run_jobs(kind, a, hf, p0, p1, v_share=0, alone=False):
            turn = 0
            for job in jobs_of(kind, a, hf):
                mm(job, p0, p1)
                if p1 == passes_of(job):
                    turn += v_share
                    on_v = turn >= 2
                    turn %= 2
                    drain(job, nc.vector.tensor_copy if on_v else nc.scalar.copy, alone)

        for i in S_INT[-1]:
            inter(i, nc.scalar.copy)
        for c in range(16):
            mul_cos(c)
            mul_sin(c, 0, 448)
            if c >= 1:
                quant_d(c - 1)
            if c % 2 == 0 and c >= 4:
                quant_dt((c - 4) // 2, 0, 2)
            for i in V_INT.get(c, []):
                inter(i, nc.vector.tensor_copy)
            for i in Q_INT.get(c, []):
                quant_m(i)
            mul_sin(c, 448, 512)
            if c < 15:
                add(c, 0, 2, nc.gpsimd)
            else:
                add(c, 0, 1, nc.gpsimd)
                add(c, 1, 2, nc.vector)
            for i in S_INT.get(c, []):
                inter(i, nc.scalar.copy)
            for k, a, hf, p0, p1 in PE.get(c, []):
                run_jobs(k, a, hf, p0, p1, 1 if c >= V_OUT_FROM else 0)
            if c % 2 == 0 and c >= 2:
                for jj in range(2):
                    flip(c // 2 - 1, jj)
                for jj in range(2):
                    unflip(c // 2 - 1, jj, nc.scalar.copy)
        quant_dt(6, 0, 2)
        quant_d(15)
        flip(7, 0)
        flip(7, 1)
        unflip(7, 0, nc.scalar.copy)
        unflip(7, 1, nc.vector.tensor_copy)
        run_jobs("W", 3, 0, 0, 2, 1, True)
        run_jobs("X", 1, 0, 0, 3)
        quant_dt(7, 0, 1)
        quant_dt(7, 1, 2)
        run_jobs("W", 3, 1, 0, 2, 1, True)
        run_jobs("X", 1, 0, 3, 4, 1)
        run_jobs("X", 1, 1, 0, 4, 1)
